import numpy as np
import ml_dtypes


def mxq(x, axis, fmt="e4m3"):
    dtype, down = {"e4m3": (ml_dtypes.float8_e4m3fn, 7), "e5m2": (ml_dtypes.float8_e5m2, 14)}[fmt]
    v = np.moveaxis(np.asarray(x, np.float32).astype(ml_dtypes.bfloat16).astype(np.float64), axis, -1)
    blocks = v.reshape(v.shape[:-1] + (-1, 32))
    amax = np.abs(blocks).max(-1, keepdims=True)
    byte = np.maximum(np.where(amax > 0, np.frexp(amax)[1] - 1 + 127, 0) - down, 1)
    scale = np.exp2(byte - 127.0)
    codes = (blocks / scale).astype(np.float32).astype(dtype).astype(np.float64)
    return np.moveaxis((codes * scale).reshape(v.shape), -1, axis)


BF16 = ml_dtypes.bfloat16


def bf(x):
    return np.asarray(x, np.float32).astype(BF16)


def f64(x):
    return np.asarray(x).astype(np.float64)


N, D, K = 2048, 512, 2048
S = 5.0


def setup_inputs():
    m = np.random.standard_normal(D) / np.sqrt(D)
    return {"data": bf(m + np.random.standard_normal((N, D)) * 0.4 / np.sqrt(D)),
            "centers": bf(m + np.random.standard_normal((K, D)) * 0.4 / np.sqrt(D))}


def reference(data, centers):
    data, centers = f64(data), f64(centers)
    x2 = np.sum(data * data, axis=-1, keepdims=True)
    c2 = np.sum(centers * centers, axis=-1)[None, :]
    xc = mxq(data, 1, "e4m3") @ mxq(centers, 1, "e4m3").T
    r2 = x2 + c2 - 2.0 * xc
    rbfs = np.exp(-S * r2)
    ones = np.ones((data.shape[0], 1))
    return np.concatenate([ones, data, rbfs], axis=-1)

@@ -1,0 +1,226 @@
+from contextlib import ExitStack
+
+import concourse.mybir as mybir
+from concourse.masks import make_identity
+
+F32 = mybir.dt.float32
+BF16 = mybir.dt.bfloat16
+U32 = mybir.dt.uint32
+U8 = mybir.dt.uint8
+FP8X4 = mybir.dt.float8_e4m3fn_x4
+ACT = mybir.ActivationFunctionType
+ALU = mybir.AluOpType
+
+P = 128
+N_ROWS = 2048
+D = 512
+N_CENTERS = 2048
+TILES = 16
+CHUNK = 4
+COLS = 1 + D + N_CENTERS
+RBF0 = 1 + D
+NB = 512
+BLOCKS = N_CENTERS // NB
+WORDS = D // 2
+ALIGN = 8
+
+FLOPS = 2 * N_ROWS * N_CENTERS * D
+
+
+def plan_units(units):
+    spans = []
+    for order, (t, j0, j1) in enumerate(units):
+        start = t * COLS + (0 if j0 < 0 else RBF0 + NB * j0)
+        end = t * COLS + RBF0 + NB * j1
+        spans.append((start, end, order))
+    by_start = sorted(spans)
+    cut_left = {}
+    cut_right = {}
+    for i, (start, end, order) in enumerate(by_start):
+        if i == 0:
+            cut_left[order] = start
+        if i == len(by_start) - 1:
+            cut_right[order] = end
+        else:
+            nxt = by_start[i + 1]
+            assert nxt[0] == end
+            if order < nxt[2]:
+                cut = (end // ALIGN) * ALIGN
+            else:
+                cut = ((end + ALIGN - 1) // ALIGN) * ALIGN
+            cut_right[order] = cut
+            cut_left[nxt[2]] = cut
+    plans = []
+    for order, (t, j0, j1) in enumerate(units):
+        exp_lo = t * COLS + RBF0 if j0 <= 0 else cut_left[order]
+        exp_hi = (t + 1) * COLS if j1 == BLOCKS else cut_right[order]
+        plans.append((exp_lo, exp_hi, cut_left[order], cut_right[order]))
+    return plans
+
+
+def tile_dicgaussianrbf_kernel(tc, data, centers, out):
+    nc = tc.nc
+    with ExitStack() as ctx:
+        keep = ctx.enter_context(tc.tile_pool(name="keep", bufs=1))
+        stage = ctx.enter_context(tc.tile_pool(name="stage", bufs=2))
+        ps_t = ctx.enter_context(tc.psum_pool(name="ps_t", bufs=3))
+        ps_c = ctx.enter_context(tc.psum_pool(name="ps_c", bufs=1))
+        ps_a = ctx.enter_context(tc.psum_pool(name="ps_a", bufs=4))
+
+        out_sb = keep.tile([P, TILES * COLS], F32, name="out_sb")
+        rows = out_sb[:].rearrange("p (t c) -> p t c", c=COLS)
+        out_flat = out.rearrange("(p t) c -> p (t c)", t=TILES)
+        x_sb = keep.tile([P, TILES * D], BF16, name="x_sb")
+        c_sb = keep.tile([P, TILES * D], BF16, name="c_sb")
+        x_codes = keep.tile([P, N_ROWS], U32, name="x_codes", align_bytes=64)
+        x_scales = keep.tile([P, N_ROWS], U8, name="x_scales", align_bytes=64)
+        c_codes = keep.tile([P, N_CENTERS], U32, name="c_codes", align_bytes=64)
+        c_scales = keep.tile([P, N_CENTERS], U8, name="c_scales", align_bytes=64)
+        c2h = keep.tile([P, N_CENTERS], F32, name="c2h")
+        ident = keep.tile([P, P], F32, name="ident")
+        warm = keep.tile([P, 1], F32, name="warm")
+        junk_s = keep.tile([P, D], BF16, name="junk_s")
+        junk_v = keep.tile([P, D], F32, name="junk_v")
+        sq = {}
+        for who in ("xs", "xv", "cs", "cv", "bs", "bv"):
+            sq[who] = keep.tile([P, TILES // 2], F32, name="sq_" + who)
+
+        c_dram = centers.rearrange("(t p) d -> p t d", p=P)
+        x_dram = data.rearrange("(p t) d -> p t d", t=TILES)
+        c_view = c_sb[:].rearrange("p (t d) -> p t d", d=D)
+        x_view = x_sb[:].rearrange("p (t d) -> p t d", d=D)
+        for c in range(TILES // CHUNK):
+            sl = slice(CHUNK * c, CHUNK * (c + 1))
+            nc.sync.dma_start(out=c_view[:, sl, :], in_=c_dram[:, sl, :])
+        for c in range(TILES // CHUNK):
+            sl = slice(CHUNK * c, CHUNK * (c + 1))
+            nc.sync.dma_start(out=x_view[:, sl, :], in_=x_dram[:, sl, :])
+
+        make_identity(nc, ident[:])
+        nc.vector.memset(warm[:], 0.0)
+        nc.scalar.activation(out=warm[:], in_=warm[:], func=ACT.Exp)
+        nc.vector.memset(rows[:, :, 0:1], 1.0)
+
+        def transpose_half(src, c, half, g32, on_vector=False):
+            src32 = src[:].bitcast(F32)
+            xt = ps_t.tile([P, 2, 2, P], F32, name="xt")
+            for a in range(2):
+                t = CHUNK * c + 2 * half + a
+                for u in range(2):
+                    lo = WORDS * t + P * u
+                    nc.tensor.transpose(xt[:, a, u, :], src32[:, lo : lo + P], ident[:])
+            dst = g32[:, 512 * half : 512 * (half + 1)].rearrange("w (a p u) -> w a p u", a=2, u=2)
+            if on_vector:
+                nc.vector.tensor_copy(out=dst, in_=xt[:].rearrange("w a u p -> w a p u"))
+            else:
+                nc.scalar.copy(out=dst, in_=xt[:].rearrange("w a u p -> w a p u"))
+
+        def quantise(g32, codes, scales, c):
+            sl = slice(NB * c, NB * (c + 1))
+            nc.vector.quantize_mx(
+                out=codes[:, sl].bitcast(FP8X4), scales=scales[:, sl], in_=g32[:].bitcast(BF16)
+            )
+
+        def sq_col(kind, t):
+            col = 2 * (t // CHUNK) + t % 2
+            return sq[kind + ("s" if t % CHUNK < 2 else "v")][:, col : col + 1]
+
+        def sumsq(view, t, kind):
+            if t % CHUNK < 2:
+                nc.scalar.activation(
+                    out=junk_s[:], in_=view[:, t, :], func=ACT.Square, accum_out=sq_col(kind, t)
+                )
+            else:
+                nc.vector.scalar_tensor_tensor(
+                    out=junk_v[:], in0=view[:, t, :], scalar=1.0, in1=view[:, t, :],
+                    op0=ALU.mult, op1=ALU.mult, accum_out=sq_col(kind, t),
+                )
+
+        def prep_centers(c):
+            g32 = stage.tile([P, 2 * NB], F32, name="g32", align_bytes=64)
+            transpose_half(c_sb, c, 0, g32)
+            transpose_half(c_sb, c, 1, g32, on_vector=True)
+            for i in range(CHUNK):
+                sumsq(c_view, CHUNK * c + i, "c")
+            quantise(g32, c_codes, c_scales, c)
+
+        def spread_c2(c):
+            c2ps = ps_c.tile([P, NB], F32, name="c2ps")
+            for i in range(CHUNK):
+                nc.tensor.matmul(
+                    out=c2ps[:, P * i : P * (i + 1)],
+                    lhsT=sq_col("c", CHUNK * c + i).to_broadcast([P, P]),
+                    rhs=ident[:], start=True, stop=True,
+                )
+            nc.scalar.mul(out=c2h[:, NB * c : NB * (c + 1)], in_=c2ps[:], mul=0.5)
+
+        x_stage = {}
+
+        def prep_data(c, part):
+            sl = slice(CHUNK * c, CHUNK * (c + 1))
+            if part == 0:
+                x_stage[c] = stage.tile([P, 2 * NB], F32, name="g32", align_bytes=64)
+                transpose_half(x_sb, c, 0, x_stage[c])
+            elif part == 1:
+                transpose_half(x_sb, c, 1, x_stage[c])
+                sumsq(x_view, CHUNK * c, "x")
+                sumsq(x_view, CHUNK * c + 1, "x")
+            else:
+                quantise(x_stage[c], x_codes, x_scales, c)
+                sumsq(x_view, CHUNK * c + 2, "x")
+                sumsq(x_view, CHUNK * c + 3, "x")
+                two = slice(2 * c, 2 * c + 2)
+                nc.scalar.mul(out=sq["bs"][:, two], in_=sq["xs"][:, two], mul=-5.0)
+                nc.vector.tensor_scalar_mul(out=sq["bv"][:, two], in0=sq["xv"][:, two], scalar1=-5.0)
+
+        def widen_data(c):
+            sl = slice(CHUNK * c, CHUNK * (c + 1))
+            nc.vector.tensor_copy(out=rows[:, sl, 1:RBF0], in_=x_view[:, sl, :])
+
+        def run_unit(unit, plan):
+            t, j0, j1 = unit
+            exp_lo, exp_hi, st_lo, st_hi = plan
+            if j0 < 0:
+                nc.sync.dma_start(out=out_flat[:, st_lo:st_hi], in_=out_sb[:, st_lo:st_hi])
+                return
+            for j in range(j0, j1):
+                acc = ps_a.tile([P, NB], F32, name="acc")
+                nc.tensor.matmul_mx(
+                    out=acc[:],
+                    lhsT=x_codes[:, P * t : P * (t + 1)].bitcast(FP8X4),
+                    lhsT_scale=x_scales[:, P * t : P * (t + 1)],
+                    rhs=c_codes[:, NB * j : NB * (j + 1)].bitcast(FP8X4),
+                    rhs_scale=c_scales[:, NB * j : NB * (j + 1)],
+                    start=True, stop=True,
+                )
+                lo = RBF0 + NB * j
+                nc.vector.tensor_tensor(
+                    out=rows[:, t, lo : lo + NB], in0=acc[:], in1=c2h[:, NB * j : NB * (j + 1)],
+                    op=ALU.subtract,
+                )
+            nc.scalar.activation(
+                out=out_sb[:, exp_lo:exp_hi], in_=out_sb[:, exp_lo:exp_hi], func=ACT.Exp,
+                bias=sq_col("b", t), scale=10.0,
+            )
+            nc.sync.dma_start(out=out_flat[:, st_lo:st_hi], in_=out_sb[:, st_lo:st_hi])
+
+        units = [(t, -1, 0) for t in range(TILES)]
+        units += [(t, 0, BLOCKS) for t in range(TILES - 1)]
+        units += [(TILES - 1, j, j + 1) for j in range(BLOCKS)]
+        plans = plan_units(units)
+
+        for c in range(TILES // CHUNK):
+            prep_centers(c)
+            if c > 0:
+                spread_c2(c - 1)
+        for part in range(3):
+            prep_data(0, part)
+        spread_c2(TILES // CHUNK - 1)
+        for i, unit in enumerate(units):
+            t = unit[0]
+            if unit[1] < 0 and t % CHUNK == 0:
+                widen_data(t // CHUNK)
+            run_unit(unit, plans[i])
+            nxt = t // CHUNK + 1
+            if unit[1] == 0 and unit[2] == BLOCKS and t % CHUNK < 3 and nxt < TILES // CHUNK:
+                prep_data(nxt, t % CHUNK)

@@ -23,6 +23,7 @@ NB = 512
 BLOCKS = N_CENTERS // NB
 WORDS = D // 2
 ALIGN = 8
+EDGE = 16
 
 FLOPS = 2 * N_ROWS * N_CENTERS * D
 
@@ -63,15 +64,14 @@ def tile_dicgaussianrbf_kernel(tc, data, centers, out):
     with ExitStack() as ctx:
         keep = ctx.enter_context(tc.tile_pool(name="keep", bufs=1))
         stage = ctx.enter_context(tc.tile_pool(name="stage", bufs=2))
+        early = ctx.enter_context(tc.tile_pool(name="early", bufs=4))
         ps_t = ctx.enter_context(tc.psum_pool(name="ps_t", bufs=3))
-        ps_c = ctx.enter_context(tc.psum_pool(name="ps_c", bufs=1))
-        ps_a = ctx.enter_context(tc.psum_pool(name="ps_a", bufs=4))
+        ps_a = ctx.enter_context(tc.psum_pool(name="ps_a", bufs=5))
 
         out_sb = keep.tile([P, TILES * COLS], F32, name="out_sb")
         rows = out_sb[:].rearrange("p (t c) -> p t c", c=COLS)
         out_flat = out.rearrange("(p t) c -> p (t c)", t=TILES)
         x_sb = keep.tile([P, TILES * D], BF16, name="x_sb")
-        c_sb = keep.tile([P, TILES * D], BF16, name="c_sb")
         x_codes = keep.tile([P, N_ROWS], U32, name="x_codes", align_bytes=64)
         x_scales = keep.tile([P, N_ROWS], U8, name="x_scales", align_bytes=64)
         c_codes = keep.tile([P, N_CENTERS], U32, name="c_codes", align_bytes=64)
@@ -80,147 +80,332 @@ def tile_dicgaussianrbf_kernel(tc, data, centers, out):
         ident = keep.tile([P, P], F32, name="ident")
         warm = keep.tile([P, 1], F32, name="warm")
         junk_s = keep.tile([P, D], BF16, name="junk_s")
-        junk_v = keep.tile([P, D], F32, name="junk_v")
-        sq = {}
-        for who in ("xs", "xv", "cs", "cv", "bs", "bv"):
-            sq[who] = keep.tile([P, TILES // 2], F32, name="sq_" + who)
+        junk_v = keep.tile([P, D], BF16, name="junk_v")
+        half = keep.tile([P, 1], F32, name="half")
+        c2_s = keep.tile([P, TILES], F32, name="c2_s")
+        c2_v = keep.tile([P, TILES], F32, name="c2_v")
+        x2_s = keep.tile([P, CHUNK], F32, name="x2_s")
+        bias = keep.tile([P, TILES], F32, name="bias")
 
         c_dram = centers.rearrange("(t p) d -> p t d", p=P)
         x_dram = data.rearrange("(p t) d -> p t d", t=TILES)
-        c_view = c_sb[:].rearrange("p (t d) -> p t d", d=D)
+        c_in = {}
         x_view = x_sb[:].rearrange("p (t d) -> p t d", d=D)
-        for c in range(TILES // CHUNK):
-            sl = slice(CHUNK * c, CHUNK * (c + 1))
-            nc.sync.dma_start(out=c_view[:, sl, :], in_=c_dram[:, sl, :])
-        for c in range(TILES // CHUNK):
+
+        def load_centers(c):
+            c_in[c] = early.tile([P, CHUNK * D], BF16, name="early", align_bytes=64)
+            view = c_in[c][:].rearrange("p (t d) -> p t d", d=D)
+            step = CHUNK // 2 if c == 0 else CHUNK
+            for i in range(0, CHUNK, step):
+                nc.sync.dma_start(
+                    out=view[:, i : i + step, :],
+                    in_=c_dram[:, CHUNK * c + i : CHUNK * c + i + step, :],
+                )
+
+        def load_data(c):
             sl = slice(CHUNK * c, CHUNK * (c + 1))
             nc.sync.dma_start(out=x_view[:, sl, :], in_=x_dram[:, sl, :])
 
-        make_identity(nc, ident[:])
-        nc.vector.memset(warm[:], 0.0)
-        nc.scalar.activation(out=warm[:], in_=warm[:], func=ACT.Exp)
-        nc.vector.memset(rows[:, :, 0:1], 1.0)
+        def constants():
+            make_identity(nc, ident[:])
+            nc.vector.memset(warm[:], 0.0)
+            nc.vector.memset(half[:], 0.5)
+            nc.scalar.activation(out=warm[:], in_=warm[:], func=ACT.Exp)
+            nc.vector.memset(rows[:, :, 0:2], 1.0)
 
-        def transpose_half(src, c, half, g32, on_vector=False):
-            src32 = src[:].bitcast(F32)
+        banks = {}
+        staged = {}
+
+        def transpose_half(kind, c, h):
+            if kind == "c":
+                src32 = c_in[c][:].bitcast(F32)
+            else:
+                src32 = x_sb[:, CHUNK * D * c : CHUNK * D * (c + 1)].bitcast(F32)
+            if h == 0:
+                staged[kind, c] = stage.tile([P, 2 * NB], F32, name="g32", align_bytes=64)
             xt = ps_t.tile([P, 2, 2, P], F32, name="xt")
             for a in range(2):
-                t = CHUNK * c + 2 * half + a
                 for u in range(2):
-                    lo = WORDS * t + P * u
+                    lo = WORDS * (2 * h + a) + P * u
                     nc.tensor.transpose(xt[:, a, u, :], src32[:, lo : lo + P], ident[:])
-            dst = g32[:, 512 * half : 512 * (half + 1)].rearrange("w (a p u) -> w a p u", a=2, u=2)
-            if on_vector:
-                nc.vector.tensor_copy(out=dst, in_=xt[:].rearrange("w a u p -> w a p u"))
-            else:
-                nc.scalar.copy(out=dst, in_=xt[:].rearrange("w a u p -> w a p u"))
+            banks[kind, c, h] = xt
 
-        def quantise(g32, codes, scales, c):
+        def copy_half(kind, c, h, on_vector):
+            g32 = staged[kind, c]
+            dst = g32[:, NB * h : NB * (h + 1)].rearrange("w (a p u) -> w a p u", a=2, u=2)
+            src = banks[kind, c, h][:].rearrange("w a u p -> w a p u")
+            if on_vector:
+                nc.vector.tensor_copy(out=dst, in_=src)
+            else:
+                nc.scalar.copy(out=dst, in_=src)
+
+        def quantise(kind, c):
+            codes, scales = (c_codes, c_scales) if kind == "c" else (x_codes, x_scales)
             sl = slice(NB * c, NB * (c + 1))
             nc.vector.quantize_mx(
-                out=codes[:, sl].bitcast(FP8X4), scales=scales[:, sl], in_=g32[:].bitcast(BF16)
+                out=codes[:, sl].bitcast(FP8X4), scales=scales[:, sl],
+                in_=staged[kind, c][:].bitcast(BF16),
             )
 
-        def sq_col(kind, t):
-            col = 2 * (t // CHUNK) + t % 2
-            return sq[kind + ("s" if t % CHUNK < 2 else "v")][:, col : col + 1]
+        def c2_col(t):
+            return (c2_v if t in (0, 2) else c2_s)[:, t : t + 1]
 
-        def sumsq(view, t, kind):
-            if t % CHUNK < 2:
-                nc.scalar.activation(
-                    out=junk_s[:], in_=view[:, t, :], func=ACT.Square, accum_out=sq_col(kind, t)
+        def c_square_s(c, i):
+            nc.scalar.activation(
+                out=junk_s[:], in_=c_in[c][:, D * i : D * (i + 1)], func=ACT.Square,
+                accum_out=c2_col(CHUNK * c + i),
+            )
+
+        def c_square_v(c, i):
+            tile = c_in[c][:, D * i : D * (i + 1)]
+            nc.vector.scalar_tensor_tensor(
+                out=junk_v[:], in0=tile, scalar=1.0, in1=tile,
+                op0=ALU.mult, op1=ALU.mult, accum_out=c2_col(CHUNK * c + i),
+            )
+
+        def x0_square_s(i):
+            nc.scalar.activation(
+                out=junk_s[:], in_=x_view[:, i, :], func=ACT.Square, accum_out=x2_s[:, i : i + 1]
+            )
+
+        def x0_bias():
+            nc.scalar.mul(out=bias[:, 0:CHUNK], in_=x2_s[:], mul=-5.0)
+
+        spread = {}
+
+        def spread_cols(c):
+            spread[c] = ps_a.tile([P, NB], F32, name="acc")
+            for i in range(CHUNK):
+                nc.tensor.transpose(
+                    spread[c][:, P * i : P * (i + 1)],
+                    c2_col(CHUNK * c + i).to_broadcast([P, P]), ident[:],
                 )
-            else:
+
+        def c2h_cols(c):
+            nc.scalar.mul(out=c2h[:, NB * c : NB * (c + 1)], in_=spread[c][:], mul=0.5)
+
+        gram = {}
+        diag = {}
+
+        def gram_products(kind, c):
+            gb = staged[kind, c][:].bitcast(BF16).rearrange("w (i p k) -> w i p k", i=CHUNK, k=4)
+            bank = ps_a.tile([P, NB], F32, name="acc")
+            for i in range(CHUNK):
+                for k in range(4):
+                    nc.tensor.matmul(
+                        out=bank[:, P * i : P * (i + 1)], lhsT=gb[:, i, :, k], rhs=gb[:, i, :, k],
+                        start=(k == 0), stop=(k == 3),
+                    )
+            gram[kind, c] = bank
+
+        def gram_diagonals(c):
+            diag[c] = stage.tile([P, NB], F32, name="diag")
+            nc.vector.tensor_tensor(
+                out=diag[c][:].rearrange("p (i q) -> p i q", i=CHUNK),
+                in0=gram["c", c][:].rearrange("p (i q) -> p i q", i=CHUNK),
+                in1=ident[:].unsqueeze(1).to_broadcast([P, CHUNK, P]),
+                op=ALU.mult,
+            )
+
+        def spread_diag(c):
+            spread[c] = ps_a.tile([P, NB], F32, name="acc")
+            nc.tensor.matmul(
+                out=spread[c][:], lhsT=half[:].to_broadcast([P, P]), rhs=diag[c][:],
+                start=True, stop=True,
+            )
+
+        def c2h_diag(c):
+            nc.scalar.copy(out=c2h[:, NB * c : NB * (c + 1)], in_=spread[c][:])
+
+        def x_bias(c):
+            for i in range(CHUNK):
+                t = CHUNK * c + i
                 nc.vector.scalar_tensor_tensor(
-                    out=junk_v[:], in0=view[:, t, :], scalar=1.0, in1=view[:, t, :],
-                    op0=ALU.mult, op1=ALU.mult, accum_out=sq_col(kind, t),
+                    out=junk_v[:, P * i : P * (i + 1)], in0=gram["x", c][:, P * i : P * (i + 1)], scalar=-5.0,
+                    in1=ident[:], op0=ALU.mult, op1=ALU.mult, accum_out=bias[:, t : t + 1],
                 )
 
-        def prep_centers(c):
-            g32 = stage.tile([P, 2 * NB], F32, name="g32", align_bytes=64)
-            transpose_half(c_sb, c, 0, g32)
-            transpose_half(c_sb, c, 1, g32, on_vector=True)
-            for i in range(CHUNK):
-                sumsq(c_view, CHUNK * c + i, "c")
-            quantise(g32, c_codes, c_scales, c)
-
-        def spread_c2(c):
-            c2ps = ps_c.tile([P, NB], F32, name="c2ps")
-            for i in range(CHUNK):
-                nc.tensor.matmul(
-                    out=c2ps[:, P * i : P * (i + 1)],
-                    lhsT=sq_col("c", CHUNK * c + i).to_broadcast([P, P]),
-                    rhs=ident[:], start=True, stop=True,
-                )
-            nc.scalar.mul(out=c2h[:, NB * c : NB * (c + 1)], in_=c2ps[:], mul=0.5)
-
-        x_stage = {}
-
-        def prep_data(c, part):
-            sl = slice(CHUNK * c, CHUNK * (c + 1))
-            if part == 0:
-                x_stage[c] = stage.tile([P, 2 * NB], F32, name="g32", align_bytes=64)
-                transpose_half(x_sb, c, 0, x_stage[c])
-            elif part == 1:
-                transpose_half(x_sb, c, 1, x_stage[c])
-                sumsq(x_view, CHUNK * c, "x")
-                sumsq(x_view, CHUNK * c + 1, "x")
-            else:
-                quantise(x_stage[c], x_codes, x_scales, c)
-                sumsq(x_view, CHUNK * c + 2, "x")
-                sumsq(x_view, CHUNK * c + 3, "x")
-                two = slice(2 * c, 2 * c + 2)
-                nc.scalar.mul(out=sq["bs"][:, two], in_=sq["xs"][:, two], mul=-5.0)
-                nc.vector.tensor_scalar_mul(out=sq["bv"][:, two], in0=sq["xv"][:, two], scalar1=-5.0)
-
-        def widen_data(c):
+        def widen(c):
             sl = slice(CHUNK * c, CHUNK * (c + 1))
             nc.vector.tensor_copy(out=rows[:, sl, 1:RBF0], in_=x_view[:, sl, :])
 
-        def run_unit(unit, plan):
-            t, j0, j1 = unit
-            exp_lo, exp_hi, st_lo, st_hi = plan
-            if j0 < 0:
-                nc.sync.dma_start(out=out_flat[:, st_lo:st_hi], in_=out_sb[:, st_lo:st_hi])
-                return
-            for j in range(j0, j1):
-                acc = ps_a.tile([P, NB], F32, name="acc")
-                nc.tensor.matmul_mx(
-                    out=acc[:],
-                    lhsT=x_codes[:, P * t : P * (t + 1)].bitcast(FP8X4),
-                    lhsT_scale=x_scales[:, P * t : P * (t + 1)],
-                    rhs=c_codes[:, NB * j : NB * (j + 1)].bitcast(FP8X4),
-                    rhs_scale=c_scales[:, NB * j : NB * (j + 1)],
-                    start=True, stop=True,
+        def widen_g(c):
+            for t in range(CHUNK * c, CHUNK * (c + 1)):
+                nc.gpsimd.tensor_scalar(
+                    out=rows[:, t, 1 : RBF0 - EDGE // 2], in0=x_view[:, t, 0 : D - EDGE // 2],
+                    scalar1=1.0, scalar2=0.0, op0=ALU.mult, op1=ALU.add,
                 )
-                lo = RBF0 + NB * j
-                nc.vector.tensor_tensor(
-                    out=rows[:, t, lo : lo + NB], in0=acc[:], in1=c2h[:, NB * j : NB * (j + 1)],
-                    op=ALU.subtract,
-                )
-            nc.scalar.activation(
-                out=out_sb[:, exp_lo:exp_hi], in_=out_sb[:, exp_lo:exp_hi], func=ACT.Exp,
-                bias=sq_col("b", t), scale=10.0,
+
+        def widen_edge(c):
+            sl = slice(CHUNK * c, CHUNK * (c + 1))
+            nc.vector.tensor_copy(
+                out=rows[:, sl, RBF0 - EDGE : RBF0], in_=x_view[:, sl, D - EDGE : D]
             )
-            nc.sync.dma_start(out=out_flat[:, st_lo:st_hi], in_=out_sb[:, st_lo:st_hi])
+
+        acc = {}
+
+        def product(t, j):
+            acc[t, j] = ps_a.tile([P, NB], F32, name="acc")
+            nc.tensor.matmul_mx(
+                out=acc[t, j][:],
+                lhsT=x_codes[:, P * t : P * (t + 1)].bitcast(FP8X4),
+                lhsT_scale=x_scales[:, P * t : P * (t + 1)],
+                rhs=c_codes[:, NB * j : NB * (j + 1)].bitcast(FP8X4),
+                rhs_scale=c_scales[:, NB * j : NB * (j + 1)],
+                start=True, stop=True,
+            )
+
+        def minus_c2h(t, j):
+            lo = RBF0 + NB * j
+            nc.vector.tensor_tensor(
+                out=rows[:, t, lo : lo + NB], in0=acc[t, j][:], in1=c2h[:, NB * j : NB * (j + 1)],
+                op=ALU.subtract,
+            )
 
         units = [(t, -1, 0) for t in range(TILES)]
-        units += [(t, 0, BLOCKS) for t in range(TILES - 1)]
+        units += [(t, 0, 2) for t in range(CHUNK)]
+        units += [(t, 2, BLOCKS) for t in range(CHUNK)]
+        units += [(t, 0, BLOCKS) for t in range(CHUNK, TILES - 1)]
         units += [(TILES - 1, j, j + 1) for j in range(BLOCKS)]
-        plans = plan_units(units)
+        plans = dict(zip(units, plan_units(units)))
 
-        for c in range(TILES // CHUNK):
-            prep_centers(c)
-            if c > 0:
-                spread_c2(c - 1)
-        for part in range(3):
-            prep_data(0, part)
-        spread_c2(TILES // CHUNK - 1)
-        for i, unit in enumerate(units):
-            t = unit[0]
-            if unit[1] < 0 and t % CHUNK == 0:
-                widen_data(t // CHUNK)
-            run_unit(unit, plans[i])
-            nxt = t // CHUNK + 1
-            if unit[1] == 0 and unit[2] == BLOCKS and t % CHUNK < 3 and nxt < TILES // CHUNK:
-                prep_data(nxt, t % CHUNK)
+        def exponentiate(t, j0, j1):
+            lo, hi = plans[t, j0, j1][:2]
+            nc.scalar.activation(
+                out=out_sb[:, lo:hi], in_=out_sb[:, lo:hi], func=ACT.Exp,
+                bias=bias[:, t : t + 1], scale=10.0,
+            )
+
+        def store(t, j0, j1):
+            lo, hi = plans[t, j0, j1][2:]
+            nc.sync.dma_start(out=out_flat[:, lo:hi], in_=out_sb[:, lo:hi])
+
+        def store_data(c):
+            for t in range(CHUNK * c, CHUNK * (c + 1)):
+                store(t, -1, 0)
+
+        first = range(CHUNK)
+
+        with tc.manual_schedule():
+            load_centers(0)
+            load_data(0)
+            for c in (1, 2, 3):
+                load_centers(c)
+            for c in (1, 2, 3):
+                load_data(c)
+            constants()
+
+            transpose_half("c", 0, 0)
+            transpose_half("c", 0, 1)
+            c_square_v(0, 0)
+            c_square_s(0, 1)
+            c_square_v(0, 2)
+            copy_half("c", 0, 0, False)
+            copy_half("c", 0, 1, True)
+            c_square_s(0, 3)
+            transpose_half("x", 0, 0)
+            transpose_half("x", 0, 1)
+            quantise("c", 0)
+            copy_half("x", 0, 0, False)
+            copy_half("x", 0, 1, True)
+            widen_g(0)
+            spread_cols(0)
+            quantise("x", 0)
+            transpose_half("c", 1, 0)
+            transpose_half("c", 1, 1)
+            c2h_cols(0)
+            widen_g(1)
+            copy_half("c", 1, 0, False)
+            copy_half("c", 1, 1, True)
+            for i in range(CHUNK):
+                c_square_s(1, i)
+            for t in first:
+                product(t, 0)
+            quantise("c", 1)
+            widen_edge(0)
+            store_data(0)
+            transpose_half("c", 2, 0)
+            transpose_half("c", 2, 1)
+            copy_half("c", 2, 0, False)
+            spread_cols(1)
+            c2h_cols(1)
+            for t in first:
+                minus_c2h(t, 0)
+                x0_square_s(t)
+            x0_bias()
+            copy_half("c", 2, 1, True)
+            widen_edge(1)
+            store_data(1)
+            widen_g(2)
+            quantise("c", 2)
+            gram_products("c", 2)
+            for t in first:
+                product(t, 1)
+            transpose_half("c", 3, 0)
+            transpose_half("c", 3, 1)
+            copy_half("c", 3, 0, False)
+            for t in first:
+                minus_c2h(t, 1)
+                exponentiate(t, 0, 2)
+                store(t, 0, 2)
+                if t == 1:
+                    gram_diagonals(2)
+                    spread_diag(2)
+                    c2h_diag(2)
+            widen_edge(2)
+            store_data(2)
+            widen_g(3)
+            copy_half("c", 3, 1, True)
+            quantise("c", 3)
+            gram_products("c", 3)
+            for t in first:
+                product(t, 2)
+            for t in first:
+                minus_c2h(t, 2)
+                if t == 1:
+                    gram_diagonals(3)
+                    transpose_half("x", 1, 0)
+                    transpose_half("x", 1, 1)
+                    spread_diag(3)
+                    copy_half("x", 1, 0, False)
+                    copy_half("x", 1, 1, False)
+                    c2h_diag(3)
+            widen_edge(3)
+            quantise("x", 1)
+            store_data(3)
+            for t in first:
+                product(t, 3)
+            for t in first:
+                minus_c2h(t, 3)
+                exponentiate(t, 2, BLOCKS)
+                store(t, 2, BLOCKS)
+            gram_products("x", 1)
+            x_bias(1)
+
+            for t in range(CHUNK, TILES):
+                nxt = t // CHUNK + 1
+                more = nxt < TILES // CHUNK
+                part = t % CHUNK
+                if more and part == 0:
+                    transpose_half("x", nxt, 0)
+                    transpose_half("x", nxt, 1)
+                for j in range(BLOCKS):
+                    product(t, j)
+                if more and part == 0:
+                    copy_half("x", nxt, 0, False)
+                if more and part == 1:
+                    copy_half("x", nxt, 1, False)
+                if more and part == 2:
+                    gram_products("x", nxt)
+                for j in range(BLOCKS):
+                    minus_c2h(t, j)
+                    if t == TILES - 1:
+                        exponentiate(t, j, j + 1)
+                        store(t, j, j + 1)
+                    if more and part == 2 and j == 1:
+                        quantise("x", nxt)
+                if more and part == 3:
+                    x_bias(nxt)
+                if t < TILES - 1:
+                    exponentiate(t, 0, BLOCKS)
+                    store(t, 0, BLOCKS)

@@ -23,7 +23,6 @@ NB = 512
 BLOCKS = N_CENTERS // NB
 WORDS = D // 2
 ALIGN = 8
-EDGE = 16
 
 FLOPS = 2 * N_ROWS * N_CENTERS * D
 
@@ -68,8 +67,9 @@ def tile_dicgaussianrbf_kernel(tc, data, centers, out):
         ps_t = ctx.enter_context(tc.psum_pool(name="ps_t", bufs=3))
         ps_a = ctx.enter_context(tc.psum_pool(name="ps_a", bufs=5))
 
-        out_sb = keep.tile([P, TILES * COLS], F32, name="out_sb")
-        rows = out_sb[:].rearrange("p (t c) -> p t c", c=COLS)
+        out_tile = keep.tile([P, ALIGN + TILES * COLS], F32, name="out_tile")
+        out_sb = out_tile[:, ALIGN : ALIGN + TILES * COLS]
+        rows = out_sb.rearrange("p (t c) -> p t c", c=COLS)
         out_flat = out.rearrange("(p t) c -> p (t c)", t=TILES)
         x_sb = keep.tile([P, TILES * D], BF16, name="x_sb")
         x_codes = keep.tile([P, N_ROWS], U32, name="x_codes", align_bytes=64)
@@ -82,6 +82,7 @@ def tile_dicgaussianrbf_kernel(tc, data, centers, out):
         junk_s = keep.tile([P, D], BF16, name="junk_s")
         junk_v = keep.tile([P, D], BF16, name="junk_v")
         half = keep.tile([P, 1], F32, name="half")
+        fence = keep.tile([P, 1], U32, name="fence")
         c2_s = keep.tile([P, TILES], F32, name="c2_s")
         c2_v = keep.tile([P, TILES], F32, name="c2_v")
         x2_s = keep.tile([P, CHUNK], F32, name="x2_s")
@@ -111,7 +112,7 @@ def tile_dicgaussianrbf_kernel(tc, data, centers, out):
             nc.vector.memset(warm[:], 0.0)
             nc.vector.memset(half[:], 0.5)
             nc.scalar.activation(out=warm[:], in_=warm[:], func=ACT.Exp)
-            nc.vector.memset(rows[:, :, 0:2], 1.0)
+            nc.vector.memset(rows[:, 0:CHUNK, 0:1], 1.0)
 
         banks = {}
         staged = {}
@@ -189,7 +190,7 @@ def tile_dicgaussianrbf_kernel(tc, data, centers, out):
 
         def gram_products(kind, c):
             gb = staged[kind, c][:].bitcast(BF16).rearrange("w (i p k) -> w i p k", i=CHUNK, k=4)
-            bank = ps_a.tile([P, NB], F32, name="acc")
+            bank = ps_t.tile([P, NB], F32, name="xt")
             for i in range(CHUNK):
                 for k in range(4):
                     nc.tensor.matmul(
@@ -198,11 +199,11 @@ def tile_dicgaussianrbf_kernel(tc, data, centers, out):
                     )
             gram[kind, c] = bank
 
-        def gram_diagonals(c):
-            diag[c] = stage.tile([P, NB], F32, name="diag")
+        def gram_diagonals(kind, c):
+            diag[kind, c] = stage.tile([P, NB], F32, name="diag")
             nc.vector.tensor_tensor(
-                out=diag[c][:].rearrange("p (i q) -> p i q", i=CHUNK),
-                in0=gram["c", c][:].rearrange("p (i q) -> p i q", i=CHUNK),
+                out=diag[kind, c][:].rearrange("p (i q) -> p i q", i=CHUNK),
+                in0=gram[kind, c][:].rearrange("p (i q) -> p i q", i=CHUNK),
                 in1=ident[:].unsqueeze(1).to_broadcast([P, CHUNK, P]),
                 op=ALU.mult,
             )
@@ -210,7 +211,7 @@ def tile_dicgaussianrbf_kernel(tc, data, centers, out):
         def spread_diag(c):
             spread[c] = ps_a.tile([P, NB], F32, name="acc")
             nc.tensor.matmul(
-                out=spread[c][:], lhsT=half[:].to_broadcast([P, P]), rhs=diag[c][:],
+                out=spread[c][:], lhsT=half[:].to_broadcast([P, P]), rhs=diag["c", c][:],
                 start=True, stop=True,
             )
 
@@ -221,26 +222,28 @@ def tile_dicgaussianrbf_kernel(tc, data, centers, out):
             for i in range(CHUNK):
                 t = CHUNK * c + i
                 nc.vector.scalar_tensor_tensor(
-                    out=junk_v[:, P * i : P * (i + 1)], in0=gram["x", c][:, P * i : P * (i + 1)], scalar=-5.0,
-                    in1=ident[:], op0=ALU.mult, op1=ALU.mult, accum_out=bias[:, t : t + 1],
+                    out=junk_v[:, P * i : P * (i + 1)], in0=gram["x", c][:, P * i : P * (i + 1)],
+                    scalar=-5.0, in1=ident[:], op0=ALU.mult, op1=ALU.mult,
+                    accum_out=bias[:, t : t + 1],
                 )
 
-        def widen(c):
+        def after_quantise(kind, c):
+            codes = c_codes if kind == "c" else x_codes
+            nc.gpsimd.tensor_copy(out=fence[:], in_=codes[:, NB * c : NB * c + 1])
+
+        def widen_v(c):
             sl = slice(CHUNK * c, CHUNK * (c + 1))
             nc.vector.tensor_copy(out=rows[:, sl, 1:RBF0], in_=x_view[:, sl, :])
 
         def widen_g(c):
             for t in range(CHUNK * c, CHUNK * (c + 1)):
                 nc.gpsimd.tensor_scalar(
-                    out=rows[:, t, 1 : RBF0 - EDGE // 2], in0=x_view[:, t, 0 : D - EDGE // 2],
+                    out=rows[:, t, 1:RBF0], in0=x_view[:, t, :],
                     scalar1=1.0, scalar2=0.0, op0=ALU.mult, op1=ALU.add,
                 )
-
-        def widen_edge(c):
-            sl = slice(CHUNK * c, CHUNK * (c + 1))
-            nc.vector.tensor_copy(
-                out=rows[:, sl, RBF0 - EDGE : RBF0], in_=x_view[:, sl, D - EDGE : D]
-            )
+                lo = ALIGN - 1 + COLS * t
+                guard = out_tile[:, lo : lo + 2 * (D + 2)].rearrange("p (a b) -> p a b", a=2)
+                nc.gpsimd.memset(guard[:, :, 0:2], 1.0)
 
         acc = {}
 
@@ -263,9 +266,10 @@ def tile_dicgaussianrbf_kernel(tc, data, centers, out):
             )
 
         units = [(t, -1, 0) for t in range(TILES)]
-        units += [(t, 0, 2) for t in range(CHUNK)]
-        units += [(t, 2, BLOCKS) for t in range(CHUNK)]
-        units += [(t, 0, BLOCKS) for t in range(CHUNK, TILES - 1)]
+        units += [(t, 0, 2) for t in range(2 * CHUNK)]
+        units += [(t, 2, BLOCKS) for t in range(2 * CHUNK)]
+        for t in range(2 * CHUNK, TILES - 1):
+            units += [(t, 0, 2), (t, 2, BLOCKS)]
         units += [(TILES - 1, j, j + 1) for j in range(BLOCKS)]
         plans = dict(zip(units, plan_units(units)))
 
@@ -285,6 +289,7 @@ def tile_dicgaussianrbf_kernel(tc, data, centers, out):
                 store(t, -1, 0)
 
         first = range(CHUNK)
+        second = range(CHUNK, 2 * CHUNK)
 
         with tc.manual_schedule():
             load_centers(0)
@@ -299,113 +304,144 @@ def tile_dicgaussianrbf_kernel(tc, data, centers, out):
             transpose_half("c", 0, 1)
             c_square_v(0, 0)
             c_square_s(0, 1)
-            c_square_v(0, 2)
             copy_half("c", 0, 0, False)
             copy_half("c", 0, 1, True)
+            c_square_v(0, 2)
             c_square_s(0, 3)
             transpose_half("x", 0, 0)
             transpose_half("x", 0, 1)
             quantise("c", 0)
             copy_half("x", 0, 0, False)
             copy_half("x", 0, 1, True)
-            widen_g(0)
             spread_cols(0)
-            quantise("x", 0)
             transpose_half("c", 1, 0)
             transpose_half("c", 1, 1)
             c2h_cols(0)
-            widen_g(1)
             copy_half("c", 1, 0, False)
+            widen_v(0)
+            store_data(0)
+            quantise("x", 0)
             copy_half("c", 1, 1, True)
-            for i in range(CHUNK):
-                c_square_s(1, i)
+            c_square_s(1, 0)
+            c_square_s(1, 1)
+            transpose_half("c", 2, 0)
             for t in first:
                 product(t, 0)
-            quantise("c", 1)
-            widen_edge(0)
-            store_data(0)
-            transpose_half("c", 2, 0)
             transpose_half("c", 2, 1)
             copy_half("c", 2, 0, False)
+            c_square_s(1, 2)
+            c_square_s(1, 3)
             spread_cols(1)
             c2h_cols(1)
-            for t in first:
-                minus_c2h(t, 0)
-                x0_square_s(t)
-            x0_bias()
-            copy_half("c", 2, 1, True)
-            widen_edge(1)
+            minus_c2h(0, 0)
+            quantise("c", 1)
+            after_quantise("c", 1)
+            widen_g(1)
             store_data(1)
-            widen_g(2)
+            minus_c2h(1, 0)
+            minus_c2h(2, 0)
+            copy_half("c", 2, 1, True)
+            minus_c2h(3, 0)
             quantise("c", 2)
-            gram_products("c", 2)
+            after_quantise("c", 2)
+            widen_g(2)
+            store_data(2)
+            transpose_half("x", 1, 0)
+            transpose_half("x", 1, 1)
             for t in first:
                 product(t, 1)
+            copy_half("x", 1, 0, False)
+            for t in first:
+                x0_square_s(t)
+            x0_bias()
+            gram_products("c", 2)
             transpose_half("c", 3, 0)
             transpose_half("c", 3, 1)
+            minus_c2h(0, 1)
+            copy_half("x", 1, 1, True)
+            minus_c2h(1, 1)
+            minus_c2h(2, 1)
+            quantise("x", 1)
+            after_quantise("x", 1)
+            widen_g(3)
+            minus_c2h(3, 1)
+            gram_diagonals("c", 2)
+            for t in second:
+                product(t, 0)
+            spread_diag(2)
+            gram_products("x", 1)
             copy_half("c", 3, 0, False)
             for t in first:
-                minus_c2h(t, 1)
                 exponentiate(t, 0, 2)
                 store(t, 0, 2)
                 if t == 1:
-                    gram_diagonals(2)
-                    spread_diag(2)
                     c2h_diag(2)
-            widen_edge(2)
-            store_data(2)
-            widen_g(3)
+            store_data(3)
             copy_half("c", 3, 1, True)
+            minus_c2h(4, 0)
+            minus_c2h(5, 0)
             quantise("c", 3)
+            minus_c2h(6, 0)
+            minus_c2h(7, 0)
+            for t in second:
+                product(t, 1)
             gram_products("c", 3)
+            x_bias(1)
+            for t in second:
+                minus_c2h(t, 1)
+                exponentiate(t, 0, 2)
+                store(t, 0, 2)
+            transpose_half("x", 2, 0)
+            transpose_half("x", 2, 1)
             for t in first:
                 product(t, 2)
+            gram_diagonals("c", 3)
+            spread_diag(3)
             for t in first:
                 minus_c2h(t, 2)
-                if t == 1:
-                    gram_diagonals(3)
-                    transpose_half("x", 1, 0)
-                    transpose_half("x", 1, 1)
-                    spread_diag(3)
-                    copy_half("x", 1, 0, False)
-                    copy_half("x", 1, 1, False)
-                    c2h_diag(3)
-            widen_edge(3)
-            quantise("x", 1)
-            store_data(3)
+            c2h_diag(3)
+            copy_half("x", 2, 0, False)
+            copy_half("x", 2, 1, False)
             for t in first:
                 product(t, 3)
-            for t in first:
                 minus_c2h(t, 3)
                 exponentiate(t, 2, BLOCKS)
                 store(t, 2, BLOCKS)
-            gram_products("x", 1)
-            x_bias(1)
+            quantise("x", 2)
+            for t in second:
+                product(t, 2)
+                product(t, 3)
+                minus_c2h(t, 2)
+                minus_c2h(t, 3)
+                exponentiate(t, 2, BLOCKS)
+                store(t, 2, BLOCKS)
+                if t == 5:
+                    gram_products("x", 2)
+            x_bias(2)
 
-            for t in range(CHUNK, TILES):
+            for t in range(2 * CHUNK, TILES):
                 nxt = t // CHUNK + 1
                 more = nxt < TILES // CHUNK
                 part = t % CHUNK
-                if more and part == 0:
-                    transpose_half("x", nxt, 0)
-                    transpose_half("x", nxt, 1)
                 for j in range(BLOCKS):
                     product(t, j)
                 if more and part == 0:
+                    transpose_half("x", nxt, 0)
+                    transpose_half("x", nxt, 1)
                     copy_half("x", nxt, 0, False)
                 if more and part == 1:
                     copy_half("x", nxt, 1, False)
-                if more and part == 2:
+                if more and part == 3:
                     gram_products("x", nxt)
                 for j in range(BLOCKS):
                     minus_c2h(t, j)
                     if t == TILES - 1:
                         exponentiate(t, j, j + 1)
                         store(t, j, j + 1)
-                    if more and part == 2 and j == 1:
+                    elif j % 2 == 1:
+                        exponentiate(t, j - 1, j + 1)
+                        store(t, j - 1, j + 1)
+                    if more and part == 2 and j == 0:
                         quantise("x", nxt)
                 if more and part == 3:
                     x_bias(nxt)
-                if t < TILES - 1:
-                    exponentiate(t, 0, BLOCKS)
-                    store(t, 0, BLOCKS)

@@ -268,15 +268,21 @@ def tile_dicgaussianrbf_kernel(tc, data, centers, out):
         units = [(t, -1, 0) for t in range(TILES)]
         units += [(t, 0, 2) for t in range(2 * CHUNK)]
         units += [(t, 2, BLOCKS) for t in range(2 * CHUNK)]
-        for t in range(2 * CHUNK, TILES - 1):
-            units += [(t, 0, 2), (t, 2, BLOCKS)]
-        units += [(TILES - 1, j, j + 1) for j in range(BLOCKS)]
+        units += [(t, 0, BLOCKS) for t in range(2 * CHUNK, TILES - 1)]
+        units += [(TILES - 1, 0, 2), (TILES - 1, 2, BLOCKS)]
         plans = dict(zip(units, plan_units(units)))
 
         def exponentiate(t, j0, j1):
             lo, hi = plans[t, j0, j1][:2]
             nc.scalar.activation(
                 out=out_sb[:, lo:hi], in_=out_sb[:, lo:hi], func=ACT.Exp,
+                bias=bias[:, t : t + 1], scale=10.0,
+            )
+
+        def exponentiate_half(t, j):
+            lo = RBF0 + NB * j
+            nc.scalar.activation(
+                out=rows[:, t, lo : lo + 2 * NB], in_=rows[:, t, lo : lo + 2 * NB], func=ACT.Exp,
                 bias=bias[:, t : t + 1], scale=10.0,
             )
 
@@ -435,13 +441,14 @@ def tile_dicgaussianrbf_kernel(tc, data, centers, out):
                     gram_products("x", nxt)
                 for j in range(BLOCKS):
                     minus_c2h(t, j)
-                    if t == TILES - 1:
-                        exponentiate(t, j, j + 1)
-                        store(t, j, j + 1)
-                    elif j % 2 == 1:
+                    if j % 2 == 1 and t == TILES - 1:
                         exponentiate(t, j - 1, j + 1)
                         store(t, j - 1, j + 1)
+                    elif j % 2 == 1:
+                        exponentiate_half(t, j - 1)
                     if more and part == 2 and j == 0:
                         quantise("x", nxt)
                 if more and part == 3:
                     x_bias(nxt)
+                if t < TILES - 1:
+                    store(t, 0, BLOCKS)

@@ -22,7 +22,8 @@ RBF0 = 1 + D
 NB = 512
 BLOCKS = N_CENTERS // NB
 WORDS = D // 2
-ALIGN = 8
+ALIGN = 16
+PAD = 64
 
 FLOPS = 2 * N_ROWS * N_CENTERS * D
 
@@ -67,8 +68,8 @@ def tile_dicgaussianrbf_kernel(tc, data, centers, out):
         ps_t = ctx.enter_context(tc.psum_pool(name="ps_t", bufs=3))
         ps_a = ctx.enter_context(tc.psum_pool(name="ps_a", bufs=5))
 
-        out_tile = keep.tile([P, ALIGN + TILES * COLS], F32, name="out_tile")
-        out_sb = out_tile[:, ALIGN : ALIGN + TILES * COLS]
+        out_tile = keep.tile([P, PAD + TILES * COLS], F32, name="out_tile", align_bytes=256)
+        out_sb = out_tile[:, PAD : PAD + TILES * COLS]
         rows = out_sb.rearrange("p (t c) -> p t c", c=COLS)
         out_flat = out.rearrange("(p t) c -> p (t c)", t=TILES)
         x_sb = keep.tile([P, TILES * D], BF16, name="x_sb")
@@ -88,20 +89,19 @@ def tile_dicgaussianrbf_kernel(tc, data, centers, out):
         x2_s = keep.tile([P, CHUNK], F32, name="x2_s")
         bias = keep.tile([P, TILES], F32, name="bias")
 
-        c_dram = centers.rearrange("(t p) d -> p t d", p=P)
+        c_dram = centers.rearrange("(c h p i) d -> p c h (i d)", c=TILES // CHUNK, h=2, i=2)
         x_dram = data.rearrange("(p t) d -> p t d", t=TILES)
         c_in = {}
         x_view = x_sb[:].rearrange("p (t d) -> p t d", d=D)
 
         def load_centers(c):
             c_in[c] = early.tile([P, CHUNK * D], BF16, name="early", align_bytes=64)
-            view = c_in[c][:].rearrange("p (t d) -> p t d", d=D)
-            step = CHUNK // 2 if c == 0 else CHUNK
-            for i in range(0, CHUNK, step):
-                nc.sync.dma_start(
-                    out=view[:, i : i + step, :],
-                    in_=c_dram[:, CHUNK * c + i : CHUNK * c + i + step, :],
-                )
+            view = c_in[c][:].rearrange("p (h n) -> p h n", h=2)
+            if c == 0:
+                for h in range(2):
+                    nc.sync.dma_start(out=view[:, h, :], in_=c_dram[:, c, h, :])
+            else:
+                nc.sync.dma_start(out=view, in_=c_dram[:, c, :, :])
 
         def load_data(c):
             sl = slice(CHUNK * c, CHUNK * (c + 1))
@@ -112,7 +112,7 @@ def tile_dicgaussianrbf_kernel(tc, data, centers, out):
             nc.vector.memset(warm[:], 0.0)
             nc.vector.memset(half[:], 0.5)
             nc.scalar.activation(out=warm[:], in_=warm[:], func=ACT.Exp)
-            nc.vector.memset(rows[:, 0:CHUNK, 0:1], 1.0)
+            nc.vector.memset(rows[:, :, 0:2], 1.0)
 
         banks = {}
         staged = {}
@@ -132,9 +132,13 @@ def tile_dicgaussianrbf_kernel(tc, data, centers, out):
             banks[kind, c, h] = xt
 
         def copy_half(kind, c, h, on_vector):
-            g32 = staged[kind, c]
-            dst = g32[:, NB * h : NB * (h + 1)].rearrange("w (a p u) -> w a p u", a=2, u=2)
-            src = banks[kind, c, h][:].rearrange("w a u p -> w a p u")
+            half = staged[kind, c][:, NB * h : NB * (h + 1)]
+            if kind == "c":
+                dst = half.rearrange("w (p a u) -> w p a u", a=2, u=2)
+                src = banks[kind, c, h][:].rearrange("w a u p -> w p a u")
+            else:
+                dst = half.rearrange("w (a p u) -> w a p u", a=2, u=2)
+                src = banks[kind, c, h][:].rearrange("w a u p -> w a p u")
             if on_vector:
                 nc.vector.tensor_copy(out=dst, in_=src)
             else:
@@ -183,7 +187,10 @@ def tile_dicgaussianrbf_kernel(tc, data, centers, out):
                 )
 
         def c2h_cols(c):
-            nc.scalar.mul(out=c2h[:, NB * c : NB * (c + 1)], in_=spread[c][:], mul=0.5)
+            nc.scalar.mul(
+                out=c2h[:, NB * c : NB * (c + 1)].rearrange("q (h p a) -> q h p a", h=2, a=2),
+                in_=spread[c][:].rearrange("q (h a p) -> q h p a", h=2, a=2), mul=0.5,
+            )
 
         gram = {}
         diag = {}
@@ -241,9 +248,9 @@ def tile_dicgaussianrbf_kernel(tc, data, centers, out):
                     out=rows[:, t, 1:RBF0], in0=x_view[:, t, :],
                     scalar1=1.0, scalar2=0.0, op0=ALU.mult, op1=ALU.add,
                 )
-                lo = ALIGN - 1 + COLS * t
-                guard = out_tile[:, lo : lo + 2 * (D + 2)].rearrange("p (a b) -> p a b", a=2)
-                nc.gpsimd.memset(guard[:, :, 0:2], 1.0)
+            lo = PAD - 1 + COLS * CHUNK * c
+            guard = out_tile[:, lo : lo + CHUNK * COLS].rearrange("p (t c) -> p t c", c=COLS)
+            nc.gpsimd.memset(guard[:, :, 0 : D + 3 : D + 2], 1.0)
 
         acc = {}
 
@@ -351,7 +358,6 @@ def tile_dicgaussianrbf_kernel(tc, data, centers, out):
             quantise("c", 2)
             after_quantise("c", 2)
             widen_g(2)
-            store_data(2)
             transpose_half("x", 1, 0)
             transpose_half("x", 1, 1)
             for t in first:
@@ -378,11 +384,11 @@ def tile_dicgaussianrbf_kernel(tc, data, centers, out):
             gram_products("x", 1)
             copy_half("c", 3, 0, False)
             for t in first:
+                store(t + 2 * CHUNK, -1, 0)
                 exponentiate(t, 0, 2)
                 store(t, 0, 2)
                 if t == 1:
                     c2h_diag(2)
-            store_data(3)
             copy_half("c", 3, 1, True)
             minus_c2h(4, 0)
             minus_c2h(5, 0)
@@ -397,6 +403,7 @@ def tile_dicgaussianrbf_kernel(tc, data, centers, out):
                 minus_c2h(t, 1)
                 exponentiate(t, 0, 2)
                 store(t, 0, 2)
+                store(t + 2 * CHUNK, -1, 0)
             transpose_half("x", 2, 0)
             transpose_half("x", 2, 1)
             for t in first:

@@ -112,7 +112,7 @@ def tile_dicgaussianrbf_kernel(tc, data, centers, out):
             nc.vector.memset(warm[:], 0.0)
             nc.vector.memset(half[:], 0.5)
             nc.scalar.activation(out=warm[:], in_=warm[:], func=ACT.Exp)
-            nc.vector.memset(rows[:, :, 0:2], 1.0)
+            nc.vector.memset(rows[:, 0:CHUNK, 0:1], 1.0)
 
         banks = {}
         staged = {}
@@ -248,9 +248,9 @@ def tile_dicgaussianrbf_kernel(tc, data, centers, out):
                     out=rows[:, t, 1:RBF0], in0=x_view[:, t, :],
                     scalar1=1.0, scalar2=0.0, op0=ALU.mult, op1=ALU.add,
                 )
-            lo = PAD - 1 + COLS * CHUNK * c
-            guard = out_tile[:, lo : lo + CHUNK * COLS].rearrange("p (t c) -> p t c", c=COLS)
-            nc.gpsimd.memset(guard[:, :, 0 : D + 3 : D + 2], 1.0)
+                lo = PAD - 1 + COLS * t
+                guard = out_tile[:, lo : lo + 2 * (D + 2)].rearrange("p (a b) -> p a b", a=2)
+                nc.gpsimd.memset(guard[:, :, 0:2], 1.0)
 
         acc = {}
 

from contextlib import ExitStack

import concourse.mybir as mybir
from concourse.masks import make_identity

F32 = mybir.dt.float32
BF16 = mybir.dt.bfloat16
U32 = mybir.dt.uint32
U8 = mybir.dt.uint8
FP8X4 = mybir.dt.float8_e4m3fn_x4
ACT = mybir.ActivationFunctionType
ALU = mybir.AluOpType

P = 128
N_ROWS = 2048
D = 512
N_CENTERS = 2048
TILES = 16
CHUNK = 4
COLS = 1 + D + N_CENTERS
RBF0 = 1 + D
NB = 512
BLOCKS = N_CENTERS // NB
WORDS = D // 2
ALIGN = 16
PAD = 64

FLOPS = 2 * N_ROWS * N_CENTERS * D


def plan_units(units):
    spans = []
    for order, (t, j0, j1) in enumerate(units):
        start = t * COLS + (0 if j0 < 0 else RBF0 + NB * j0)
        end = t * COLS + RBF0 + NB * j1
        spans.append((start, end, order))
    by_start = sorted(spans)
    cut_left = {}
    cut_right = {}
    for i, (start, end, order) in enumerate(by_start):
        if i == 0:
            cut_left[order] = start
        if i == len(by_start) - 1:
            cut_right[order] = end
        else:
            nxt = by_start[i + 1]
            assert nxt[0] == end
            if order < nxt[2]:
                cut = (end // ALIGN) * ALIGN
            else:
                cut = ((end + ALIGN - 1) // ALIGN) * ALIGN
            cut_right[order] = cut
            cut_left[nxt[2]] = cut
    plans = []
    for order, (t, j0, j1) in enumerate(units):
        exp_lo = t * COLS + RBF0 if j0 <= 0 else cut_left[order]
        exp_hi = (t + 1) * COLS if j1 == BLOCKS else cut_right[order]
        plans.append((exp_lo, exp_hi, cut_left[order], cut_right[order]))
    return plans


def tile_dicgaussianrbf_kernel(tc, data, centers, out):
    nc = tc.nc
    with ExitStack() as ctx:
        keep = ctx.enter_context(tc.tile_pool(name="keep", bufs=1))
        stage = ctx.enter_context(tc.tile_pool(name="stage", bufs=2))
        early = ctx.enter_context(tc.tile_pool(name="early", bufs=4))
        ps_t = ctx.enter_context(tc.psum_pool(name="ps_t", bufs=3))
        ps_a = ctx.enter_context(tc.psum_pool(name="ps_a", bufs=5))

        out_tile = keep.tile([P, PAD + TILES * COLS], F32, name="out_tile", align_bytes=256)
        out_sb = out_tile[:, PAD : PAD + TILES * COLS]
        rows = out_sb.rearrange("p (t c) -> p t c", c=COLS)
        out_flat = out.rearrange("(p t) c -> p (t c)", t=TILES)
        x_sb = keep.tile([P, TILES * D], BF16, name="x_sb")
        x_codes = keep.tile([P, N_ROWS], U32, name="x_codes", align_bytes=64)
        x_scales = keep.tile([P, N_ROWS], U8, name="x_scales", align_bytes=64)
        c_codes = keep.tile([P, N_CENTERS], U32, name="c_codes", align_bytes=64)
        c_scales = keep.tile([P, N_CENTERS], U8, name="c_scales", align_bytes=64)
        c2h = keep.tile([P, N_CENTERS], F32, name="c2h")
        ident = keep.tile([P, P], F32, name="ident")
        warm = keep.tile([P, 1], F32, name="warm")
        junk_s = keep.tile([P, D], BF16, name="junk_s")
        junk_v = keep.tile([P, D], BF16, name="junk_v")
        half = keep.tile([P, 1], F32, name="half")
        fence = keep.tile([P, 1], U32, name="fence")
        c2_s = keep.tile([P, TILES], F32, name="c2_s")
        c2_v = keep.tile([P, TILES], F32, name="c2_v")
        x2_s = keep.tile([P, CHUNK], F32, name="x2_s")
        bias = keep.tile([P, TILES], F32, name="bias")

        c_dram = centers.rearrange("(c h p i) d -> p c h (i d)", c=TILES // CHUNK, h=2, i=2)
        x_dram = data.rearrange("(p t) d -> p t d", t=TILES)
        c_in = {}
        x_view = x_sb[:].rearrange("p (t d) -> p t d", d=D)

        def load_centers(c):
            c_in[c] = early.tile([P, CHUNK * D], BF16, name="early", align_bytes=64)
            view = c_in[c][:].rearrange("p (h n) -> p h n", h=2)
            if c == 0:
                for h in range(2):
                    nc.sync.dma_start(out=view[:, h, :], in_=c_dram[:, c, h, :])
            else:
                nc.sync.dma_start(out=view, in_=c_dram[:, c, :, :])

        def load_data(c):
            sl = slice(CHUNK * c, CHUNK * (c + 1))
            nc.sync.dma_start(out=x_view[:, sl, :], in_=x_dram[:, sl, :])

        def constants():
            make_identity(nc, ident[:])
            nc.vector.memset(warm[:], 0.0)
            nc.vector.memset(half[:], 0.5)
            nc.scalar.activation(out=warm[:], in_=warm[:], func=ACT.Exp)
            nc.vector.memset(rows[:, 0:CHUNK, 0:1], 1.0)

        banks = {}
        staged = {}

        def transpose_half(kind, c, h):
            if kind == "c":
                src32 = c_in[c][:].bitcast(F32)
            else:
                src32 = x_sb[:, CHUNK * D * c : CHUNK * D * (c + 1)].bitcast(F32)
            if h == 0:
                staged[kind, c] = stage.tile([P, 2 * NB], F32, name="g32", align_bytes=64)
            xt = ps_t.tile([P, 2, 2, P], F32, name="xt")
            for a in range(2):
                for u in range(2):
                    lo = WORDS * (2 * h + a) + P * u
                    nc.tensor.transpose(xt[:, a, u, :], src32[:, lo : lo + P], ident[:])
            banks[kind, c, h] = xt

        def copy_half(kind, c, h, on_vector):
            half = staged[kind, c][:, NB * h : NB * (h + 1)]
            if kind == "c":
                dst = half.rearrange("w (p a u) -> w p a u", a=2, u=2)
                src = banks[kind, c, h][:].rearrange("w a u p -> w p a u")
            else:
                dst = half.rearrange("w (a p u) -> w a p u", a=2, u=2)
                src = banks[kind, c, h][:].rearrange("w a u p -> w a p u")
            if on_vector:
                nc.vector.tensor_copy(out=dst, in_=src)
            else:
                nc.scalar.copy(out=dst, in_=src)

        def quantise(kind, c):
            codes, scales = (c_codes, c_scales) if kind == "c" else (x_codes, x_scales)
            sl = slice(NB * c, NB * (c + 1))
            nc.vector.quantize_mx(
                out=codes[:, sl].bitcast(FP8X4), scales=scales[:, sl],
                in_=staged[kind, c][:].bitcast(BF16),
            )

        def c2_col(t):
            return (c2_v if t in (0, 2) else c2_s)[:, t : t + 1]

        def c_square_s(c, i):
            nc.scalar.activation(
                out=junk_s[:], in_=c_in[c][:, D * i : D * (i + 1)], func=ACT.Square,
                accum_out=c2_col(CHUNK * c + i),
            )

        def c_square_v(c, i):
            tile = c_in[c][:, D * i : D * (i + 1)]
            nc.vector.scalar_tensor_tensor(
                out=junk_v[:], in0=tile, scalar=1.0, in1=tile,
                op0=ALU.mult, op1=ALU.mult, accum_out=c2_col(CHUNK * c + i),
            )

        def x0_square_s(i):
            nc.scalar.activation(
                out=junk_s[:], in_=x_view[:, i, :], func=ACT.Square, accum_out=x2_s[:, i : i + 1]
            )

        def x0_bias():
            nc.scalar.mul(out=bias[:, 0:CHUNK], in_=x2_s[:], mul=-5.0)

        spread = {}

        def spread_cols(c):
            spread[c] = ps_a.tile([P, NB], F32, name="acc")
            for i in range(CHUNK):
                nc.tensor.transpose(
                    spread[c][:, P * i : P * (i + 1)],
                    c2_col(CHUNK * c + i).to_broadcast([P, P]), ident[:],
                )

        def c2h_cols(c):
            nc.scalar.mul(
                out=c2h[:, NB * c : NB * (c + 1)].rearrange("q (h p a) -> q h p a", h=2, a=2),
                in_=spread[c][:].rearrange("q (h a p) -> q h p a", h=2, a=2), mul=0.5,
            )

        gram = {}
        diag = {}

        def gram_products(kind, c):
            gb = staged[kind, c][:].bitcast(BF16).rearrange("w (i p k) -> w i p k", i=CHUNK, k=4)
            bank = ps_t.tile([P, NB], F32, name="xt")
            for i in range(CHUNK):
                for k in range(4):
                    nc.tensor.matmul(
                        out=bank[:, P * i : P * (i + 1)], lhsT=gb[:, i, :, k], rhs=gb[:, i, :, k],
                        start=(k == 0), stop=(k == 3),
                    )
            gram[kind, c] = bank

        def gram_diagonals(kind, c):
            diag[kind, c] = stage.tile([P, NB], F32, name="diag")
            nc.vector.tensor_tensor(
                out=diag[kind, c][:].rearrange("p (i q) -> p i q", i=CHUNK),
                in0=gram[kind, c][:].rearrange("p (i q) -> p i q", i=CHUNK),
                in1=ident[:].unsqueeze(1).to_broadcast([P, CHUNK, P]),
                op=ALU.mult,
            )

        def spread_diag(c):
            spread[c] = ps_a.tile([P, NB], F32, name="acc")
            nc.tensor.matmul(
                out=spread[c][:], lhsT=half[:].to_broadcast([P, P]), rhs=diag["c", c][:],
                start=True, stop=True,
            )

        def c2h_diag(c):
            nc.scalar.copy(out=c2h[:, NB * c : NB * (c + 1)], in_=spread[c][:])

        def x_bias(c):
            for i in range(CHUNK):
                t = CHUNK * c + i
                nc.vector.scalar_tensor_tensor(
                    out=junk_v[:, P * i : P * (i + 1)], in0=gram["x", c][:, P * i : P * (i + 1)],
                    scalar=-5.0, in1=ident[:], op0=ALU.mult, op1=ALU.mult,
                    accum_out=bias[:, t : t + 1],
                )

        def after_quantise(kind, c):
            codes = c_codes if kind == "c" else x_codes
            nc.gpsimd.tensor_copy(out=fence[:], in_=codes[:, NB * c : NB * c + 1])

        def widen_v(c):
            sl = slice(CHUNK * c, CHUNK * (c + 1))
            nc.vector.tensor_copy(out=rows[:, sl, 1:RBF0], in_=x_view[:, sl, :])

        def widen_g(c):
            for t in range(CHUNK * c, CHUNK * (c + 1)):
                nc.gpsimd.tensor_scalar(
                    out=rows[:, t, 1:RBF0], in0=x_view[:, t, :],
                    scalar1=1.0, scalar2=0.0, op0=ALU.mult, op1=ALU.add,
                )
                lo = PAD - 1 + COLS * t
                guard = out_tile[:, lo : lo + 2 * (D + 2)].rearrange("p (a b) -> p a b", a=2)
                nc.gpsimd.memset(guard[:, :, 0:2], 1.0)

        acc = {}

        def product(t, j):
            acc[t, j] = ps_a.tile([P, NB], F32, name="acc")
            nc.tensor.matmul_mx(
                out=acc[t, j][:],
                lhsT=x_codes[:, P * t : P * (t + 1)].bitcast(FP8X4),
                lhsT_scale=x_scales[:, P * t : P * (t + 1)],
                rhs=c_codes[:, NB * j : NB * (j + 1)].bitcast(FP8X4),
                rhs_scale=c_scales[:, NB * j : NB * (j + 1)],
                start=True, stop=True,
            )

        def minus_c2h(t, j):
            lo = RBF0 + NB * j
            nc.vector.tensor_tensor(
                out=rows[:, t, lo : lo + NB], in0=acc[t, j][:], in1=c2h[:, NB * j : NB * (j + 1)],
                op=ALU.subtract,
            )

        units = [(t, -1, 0) for t in range(TILES)]
        units += [(t, 0, 2) for t in range(2 * CHUNK)]
        units += [(t, 2, BLOCKS) for t in range(2 * CHUNK)]
        units += [(t, 0, BLOCKS) for t in range(2 * CHUNK, TILES - 1)]
        units += [(TILES - 1, 0, 2), (TILES - 1, 2, BLOCKS)]
        plans = dict(zip(units, plan_units(units)))

        def exponentiate(t, j0, j1):
            lo, hi = plans[t, j0, j1][:2]
            nc.scalar.activation(
                out=out_sb[:, lo:hi], in_=out_sb[:, lo:hi], func=ACT.Exp,
                bias=bias[:, t : t + 1], scale=10.0,
            )

        def exponentiate_half(t, j):
            lo = RBF0 + NB * j
            nc.scalar.activation(
                out=rows[:, t, lo : lo + 2 * NB], in_=rows[:, t, lo : lo + 2 * NB], func=ACT.Exp,
                bias=bias[:, t : t + 1], scale=10.0,
            )

        def store(t, j0, j1):
            lo, hi = plans[t, j0, j1][2:]
            nc.sync.dma_start(out=out_flat[:, lo:hi], in_=out_sb[:, lo:hi])

        def store_data(c):
            for t in range(CHUNK * c, CHUNK * (c + 1)):
                store(t, -1, 0)

        first = range(CHUNK)
        second = range(CHUNK, 2 * CHUNK)

        with tc.manual_schedule():
            load_centers(0)
            load_data(0)
            for c in (1, 2, 3):
                load_centers(c)
            for c in (1, 2, 3):
                load_data(c)
            constants()

            transpose_half("c", 0, 0)
            transpose_half("c", 0, 1)
            c_square_v(0, 0)
            c_square_s(0, 1)
            copy_half("c", 0, 0, False)
            copy_half("c", 0, 1, True)
            c_square_v(0, 2)
            c_square_s(0, 3)
            transpose_half("x", 0, 0)
            transpose_half("x", 0, 1)
            quantise("c", 0)
            copy_half("x", 0, 0, False)
            copy_half("x", 0, 1, True)
            spread_cols(0)
            transpose_half("c", 1, 0)
            transpose_half("c", 1, 1)
            c2h_cols(0)
            copy_half("c", 1, 0, False)
            widen_v(0)
            store_data(0)
            quantise("x", 0)
            copy_half("c", 1, 1, True)
            c_square_s(1, 0)
            c_square_s(1, 1)
            transpose_half("c", 2, 0)
            for t in first:
                product(t, 0)
            transpose_half("c", 2, 1)
            copy_half("c", 2, 0, False)
            c_square_s(1, 2)
            c_square_s(1, 3)
            spread_cols(1)
            c2h_cols(1)
            minus_c2h(0, 0)
            quantise("c", 1)
            after_quantise("c", 1)
            widen_g(1)
            store_data(1)
            minus_c2h(1, 0)
            minus_c2h(2, 0)
            copy_half("c", 2, 1, True)
            minus_c2h(3, 0)
            quantise("c", 2)
            after_quantise("c", 2)
            widen_g(2)
            transpose_half("x", 1, 0)
            transpose_half("x", 1, 1)
            for t in first:
                product(t, 1)
            copy_half("x", 1, 0, False)
            for t in first:
                x0_square_s(t)
            x0_bias()
            gram_products("c", 2)
            transpose_half("c", 3, 0)
            transpose_half("c", 3, 1)
            minus_c2h(0, 1)
            copy_half("x", 1, 1, True)
            minus_c2h(1, 1)
            minus_c2h(2, 1)
            quantise("x", 1)
            after_quantise("x", 1)
            widen_g(3)
            minus_c2h(3, 1)
            gram_diagonals("c", 2)
            for t in second:
                product(t, 0)
            spread_diag(2)
            gram_products("x", 1)
            copy_half("c", 3, 0, False)
            for t in first:
                store(t + 2 * CHUNK, -1, 0)
                exponentiate(t, 0, 2)
                store(t, 0, 2)
                if t == 1:
                    c2h_diag(2)
            copy_half("c", 3, 1, True)
            minus_c2h(4, 0)
            minus_c2h(5, 0)
            quantise("c", 3)
            minus_c2h(6, 0)
            minus_c2h(7, 0)
            for t in second:
                product(t, 1)
            gram_products("c", 3)
            x_bias(1)
            for t in second:
                minus_c2h(t, 1)
                exponentiate(t, 0, 2)
                store(t, 0, 2)
                store(t + 2 * CHUNK, -1, 0)
            transpose_half("x", 2, 0)
            transpose_half("x", 2, 1)
            for t in first:
                product(t, 2)
            gram_diagonals("c", 3)
            spread_diag(3)
            for t in first:
                minus_c2h(t, 2)
            c2h_diag(3)
            copy_half("x", 2, 0, False)
            copy_half("x", 2, 1, False)
            for t in first:
                product(t, 3)
                minus_c2h(t, 3)
                exponentiate(t, 2, BLOCKS)
                store(t, 2, BLOCKS)
            quantise("x", 2)
            for t in second:
                product(t, 2)
                product(t, 3)
                minus_c2h(t, 2)
                minus_c2h(t, 3)
                exponentiate(t, 2, BLOCKS)
                store(t, 2, BLOCKS)
                if t == 5:
                    gram_products("x", 2)
            x_bias(2)

            for t in range(2 * CHUNK, TILES):
                nxt = t // CHUNK + 1
                more = nxt < TILES // CHUNK
                part = t % CHUNK
                for j in range(BLOCKS):
                    product(t, j)
                if more and part == 0:
                    transpose_half("x", nxt, 0)
                    transpose_half("x", nxt, 1)
                    copy_half("x", nxt, 0, False)
                if more and part == 1:
                    copy_half("x", nxt, 1, False)
                if more and part == 3:
                    gram_products("x", nxt)
                for j in range(BLOCKS):
                    minus_c2h(t, j)
                    if j % 2 == 1 and t == TILES - 1:
                        exponentiate(t, j - 1, j + 1)
                        store(t, j - 1, j + 1)
                    elif j % 2 == 1:
                        exponentiate_half(t, j - 1)
                    if more and part == 2 and j == 0:
                        quantise("x", nxt)
                if more and part == 3:
                    x_bias(nxt)
                if t < TILES - 1:
                    store(t, 0, BLOCKS)
